import numpy as np
import ml_dtypes


def mxq(x, axis, fmt="e4m3"):
    dtype, down = {"e4m3": (ml_dtypes.float8_e4m3fn, 7), "e5m2": (ml_dtypes.float8_e5m2, 14)}[fmt]
    v = np.moveaxis(np.asarray(x, np.float32).astype(ml_dtypes.bfloat16).astype(np.float64), axis, -1)
    blocks = v.reshape(v.shape[:-1] + (-1, 32))
    amax = np.abs(blocks).max(-1, keepdims=True)
    byte = np.maximum(np.where(amax > 0, np.frexp(amax)[1] - 1 + 127, 0) - down, 1)
    scale = np.exp2(byte - 127.0)
    codes = (blocks / scale).astype(np.float32).astype(dtype).astype(np.float64)
    return np.moveaxis((codes * scale).reshape(v.shape), -1, axis)


WIDE = False


def mx_kscale(k):
    if not WIDE:
        return np.ones(k)
    levels = np.array([10, -10, 5, -5, 0])
    a = np.random.permutation(np.resize(levels, k // 512 * 4)).reshape(k // 512, 4)
    idx = np.arange(k)
    return np.exp2(a[idx // 512, idx % 128 // 32])


BF16 = ml_dtypes.bfloat16


def bf(x):
    return np.asarray(x, np.float32).astype(BF16)


def f64(x):
    return np.asarray(x).astype(np.float64)


B, N, DIN, DH, DOUT, DIM = 4, 1024, 512, 512, 128, 512


def draw_ahat():
    g = np.random.standard_normal((N, N))
    u = np.random.standard_normal(N) * 0.5
    a = g - g.T + u[:, None] - u[None, :]
    m = (a > 0) + np.eye(N)
    dinv = 1.0 / np.sqrt(m.sum(0))
    return m * (dinv[:, None] * dinv[None, :])


def setup_inputs():
    s, t = mx_kscale(DIN), mx_kscale(N)
    r = np.random.standard_normal
    return {"x": bf((r((B, N, DIN)) * s / t[:, None]).reshape(B * N, DIN)),
            "ahat": bf(draw_ahat() * t[:, None]),
            "gcn1_w": bf(r((DIN, DH)) * 0.2 * np.sqrt(N / DIN) / s[:, None]),
            "gcn1_b": bf(r(DH) * 0.2)}


def reference(x, ahat, gcn1_w, gcn1_b):
    xb = f64(x).reshape(B, N, DIN)
    y = mxq(xb, 2, "e4m3") @ mxq(f64(gcn1_w), 0, "e4m3")
    h = (mxq(f64(ahat), 0, "e4m3").T @ mxq(y, 1, "e4m3")) + f64(gcn1_b)
    return np.maximum(h, 0.0)

@@ -1,0 +1,211 @@
+from contextlib import ExitStack
+
+import concourse.mybir as mybir
+from concourse.masks import make_identity
+
+F32 = mybir.dt.float32
+BF16 = mybir.dt.bfloat16
+U32 = mybir.dt.uint32
+U8 = mybir.dt.uint8
+FP8X4 = mybir.dt.float8_e4m3fn_x4
+
+P = 128
+PACK = 4
+K_PASS = P * PACK
+
+GRAPHS = 4
+NODES = 1024
+D_IN = 512
+D_HID = 512
+
+GROUP = K_PASS
+N_GROUPS = GRAPHS * NODES // GROUP
+PASSES = NODES // K_PASS
+F_CHUNK = 128
+F_CHUNKS = D_HID // F_CHUNK
+J_TILES = NODES // P
+N_BANKS = GRAPHS * J_TILES
+BANKS_PER_ROUND = N_BANKS // N_GROUPS
+AHEAD = 2
+LAG = 2
+
+FLOPS = 2 * GRAPHS * NODES * D_IN * D_HID + 2 * GRAPHS * NODES * NODES * D_HID
+
+
+def tile_gcn_pb_t_kernel(tc, x, ahat, gcn1_w, gcn1_b, out):
+    nc = tc.nc
+    out_rows = out.flatten_outer_dims()
+
+    with ExitStack() as stack:
+        consts = stack.enter_context(tc.tile_pool(name="consts", bufs=1))
+        adjacency = stack.enter_context(tc.tile_pool(name="adjacency", bufs=PASSES))
+        resident = stack.enter_context(tc.tile_pool(name="resident", bufs=N_GROUPS))
+        rotating = stack.enter_context(tc.tile_pool(name="rotating", bufs=3))
+        results = stack.enter_context(tc.tile_pool(name="results", bufs=2 * BANKS_PER_ROUND))
+        psum_xt = stack.enter_context(tc.psum_pool(name="psum_xt", bufs=2))
+        psum_y = stack.enter_context(tc.psum_pool(name="psum_y", bufs=3))
+        psum_out = stack.enter_context(tc.psum_pool(name="psum_out", bufs=3))
+        stack.enter_context(tc.manual_schedule())
+
+        x_raw = {}
+        x_grouped = {}
+        x_codes = {}
+        y_grouped = {}
+        y_codes = {}
+        a_raw = {}
+        a_codes = {}
+        result = {}
+
+        def load_x(g):
+            raw = resident.tile([P, PACK * D_IN], BF16, tag="x_raw")
+            nc.sync.dma_start(
+                out=raw[:], in_=x[g * GROUP : (g + 1) * GROUP, :].rearrange("(p t) k -> p (t k)", t=PACK)
+            )
+            x_raw[g] = raw
+
+        def load_adjacency(g):
+            raw = adjacency.tile([P, PACK, NODES], BF16, tag="a_raw")
+            nc.sync.dma_start(
+                out=raw[:], in_=ahat[g * K_PASS : (g + 1) * K_PASS, :].rearrange("(p t) j -> p t j", t=PACK)
+            )
+            a_raw[g] = raw
+
+        bias_row = consts.tile([P, D_HID], BF16, tag="bias_row")
+        nc.vector.memset(bias_row[:], 0.0)
+
+        load_x(0)
+        w_raw = consts.tile([P, PACK, D_HID], BF16, tag="w_raw")
+        for u in range(2):
+            nc.sync.dma_start(
+                out=w_raw[:, 2 * u : 2 * u + 2, :],
+                in_=gcn1_w[256 * u : 256 * (u + 1), :].rearrange("(q e) c -> q e c", e=2),
+            )
+        load_x(1)
+        nc.sync.dma_start(out=bias_row[0:1, :], in_=gcn1_b.unsqueeze(0))
+        for g in range(PASSES):
+            load_adjacency(g)
+            load_x(AHEAD + g)
+        for g in range(AHEAD + PASSES, N_GROUPS):
+            load_x(g)
+
+        identity = consts.tile([P, P], F32, tag="identity")
+        make_identity(nc, identity[:])
+        ones = consts.tile([P, P], BF16, tag="ones")
+        nc.vector.memset(ones[:], 1.0)
+        warm = consts.tile([P, 1], F32, tag="warm")
+        nc.vector.memset(warm[:], 0.0)
+        nc.scalar.activation(out=warm[:], in_=warm[:], func=mybir.ActivationFunctionType.Relu)
+
+        def regroup(dst, src):
+            nc.vector.tensor_copy(
+                out=dst.rearrange("p (c i) t -> p c t i", i=4), in_=src.rearrange("p t (c i) -> p c t i", i=4)
+            )
+
+        def quantise(grouped, width, pool, tag):
+            codes = pool.tile([P, width], U32, tag=tag + "_codes", align_bytes=64)
+            scales = pool.tile([P, width], U8, tag=tag + "_scales", align_bytes=64)
+            nc.vector.quantize_mx(out=codes[:].bitcast(FP8X4), scales=scales[:], in_=grouped)
+            return codes, scales
+
+        def transpose_x(g):
+            words = x_raw[g][:].bitcast(F32)
+            grouped = rotating.tile([P, PACK * GROUP], BF16, tag="x_grouped", align_bytes=64)
+            grouped_words = grouped[:].bitcast(F32)
+            for pair in range(2):
+                xt = psum_xt.tile([P, 2, 2, P], F32, tag="xt")
+                for h in range(2):
+                    for u in range(2):
+                        first = (2 * pair + h) * 256 + u * P
+                        nc.tensor.transpose(xt[:, h, u, :], words[:, first : first + P], identity[:])
+                nc.scalar.copy(
+                    out=grouped_words[:, pair * 512 : (pair + 1) * 512].rearrange(
+                        "q (h n u) -> q h n u", h=2, n=P, u=2
+                    ),
+                    in_=xt[:].rearrange("q h u n -> q h n u"),
+                )
+            x_grouped[g] = grouped
+
+        def first_matmul(g, c):
+            if c == 0:
+                grouped = rotating.tile([P, D_HID, PACK], BF16, tag="y_grouped", align_bytes=64)
+                y_grouped[g] = grouped
+            codes, scales = x_codes[g]
+            f_cols = slice(c * F_CHUNK, (c + 1) * F_CHUNK)
+            y_bank = psum_y.tile([P, PACK, F_CHUNK], F32, tag="y_bank")
+            for t in range(PACK):
+                n_cols = slice(t * P, (t + 1) * P)
+                nc.tensor.matmul_mx(
+                    out=y_bank[:, t, :],
+                    lhsT=codes[:, n_cols].bitcast(FP8X4),
+                    lhsT_scale=scales[:, n_cols],
+                    rhs=w_codes[:, f_cols].bitcast(FP8X4),
+                    rhs_scale=w_scales[:, f_cols],
+                    start=True,
+                    stop=True,
+                )
+            nc.scalar.copy(out=y_grouped[g][:, f_cols, :], in_=y_bank[:].rearrange("n t f -> n f t"))
+
+        def second_matmul(n):
+            b = n // J_TILES
+            j_cols = slice((n % J_TILES) * P, (n % J_TILES + 1) * P)
+            out_bank = psum_out.tile([P, D_HID], F32, tag="out_bank")
+            for g in range(PASSES):
+                nc.tensor.matmul_mx(
+                    out=out_bank[:],
+                    lhsT=a_codes[g][0][:, j_cols].bitcast(FP8X4),
+                    lhsT_scale=a_codes[g][1][:, j_cols],
+                    rhs=y_codes[PASSES * b + g][0][:].bitcast(FP8X4),
+                    rhs_scale=y_codes[PASSES * b + g][1][:],
+                    start=(g == 0),
+                    stop=(g == PASSES - 1),
+                )
+            biased = results.tile([P, D_HID], F32, tag="result")
+            nc.vector.tensor_tensor(out=biased[:], in0=out_bank[:], in1=bias_all[:], op=mybir.AluOpType.add)
+            result[n] = biased
+
+        def relu_and_store(n, on_vector):
+            if on_vector:
+                nc.vector.tensor_scalar_max(out=result[n][:], in0=result[n][:], scalar1=0.0)
+            else:
+                nc.scalar.activation(out=result[n][:], in_=result[n][:], func=mybir.ActivationFunctionType.Relu)
+            nc.sync.dma_start(out=out_rows[n * P : (n + 1) * P, :], in_=result[n][:])
+
+        transpose_x(0)
+        w_grouped = consts.tile([P, D_HID, PACK], BF16, tag="w_grouped", align_bytes=64)
+        regroup(w_grouped[:], w_raw[:])
+        w_codes, w_scales = quantise(w_grouped[:].rearrange("p c t -> p (c t)"), D_HID, consts, "w")
+        x_codes[0] = quantise(x_grouped[0][:], GROUP, rotating, "x")
+        transpose_x(1)
+        x_codes[1] = quantise(x_grouped[1][:], GROUP, rotating, "x")
+        bias_bank = psum_out.tile([P, D_HID], F32, tag="out_bank")
+        nc.tensor.matmul(out=bias_bank[:], lhsT=ones[:], rhs=bias_row[:], start=True, stop=True)
+        bias_all = consts.tile([P, D_HID], F32, tag="bias_all")
+        nc.scalar.copy(out=bias_all[:], in_=bias_bank[:])
+
+        for r in range(N_GROUPS + LAG):
+            first_active = r < N_GROUPS
+            banks = [BANKS_PER_ROUND * (r - LAG) + i for i in range(BANKS_PER_ROUND)] if r >= LAG else []
+            for half in range(2):
+                if first_active:
+                    first_matmul(r, 2 * half)
+                    first_matmul(r, 2 * half + 1)
+                for n in banks[2 * half : 2 * half + 2]:
+                    second_matmul(n)
+            vector_banks = [n for n in banks if first_active and n % 2 == 1]
+            for n in banks:
+                if n not in vector_banks:
+                    relu_and_store(n, on_vector=False)
+            if r + AHEAD < N_GROUPS:
+                transpose_x(r + AHEAD)
+            if r < PASSES:
+                a_grouped = adjacency.tile([P, NODES, PACK], BF16, tag="a_grouped", align_bytes=64)
+                for j_half in range(2):
+                    j_cols = slice(j_half * 512, (j_half + 1) * 512)
+                    regroup(a_grouped[:, j_cols, :], a_raw[r][:, :, j_cols])
+                a_codes[r] = quantise(a_grouped[:].rearrange("p j t -> p (j t)"), NODES, adjacency, "a")
+            if first_active:
+                y_codes[r] = quantise(y_grouped[r][:].rearrange("p f t -> p (f t)"), D_HID, resident, "y")
+            for n in vector_banks:
+                relu_and_store(n, on_vector=True)
+            if r + AHEAD < N_GROUPS:
+                x_codes[r + AHEAD] = quantise(x_grouped[r + AHEAD][:], GROUP, rotating, "x")

@@ -163,9 +163,16 @@ def tile_gcn_pb_t_kernel(tc, x, ahat, gcn1_w, gcn1_b, out):
             nc.vector.tensor_tensor(out=biased[:], in0=out_bank[:], in1=bias_all[:], op=mybir.AluOpType.add)
             result[n] = biased
 
-        def relu_and_store(n, on_vector):
-            if on_vector:
-                nc.vector.tensor_scalar_max(out=result[n][:], in0=result[n][:], scalar1=0.0)
+        def relu_and_store(n, on_gpsimd):
+            if on_gpsimd:
+                nc.gpsimd.tensor_scalar(
+                    out=result[n][:],
+                    in0=result[n][:],
+                    scalar1=0.0,
+                    scalar2=0.0,
+                    op0=mybir.AluOpType.max,
+                    op1=mybir.AluOpType.add,
+                )
             else:
                 nc.scalar.activation(out=result[n][:], in_=result[n][:], func=mybir.ActivationFunctionType.Relu)
             nc.sync.dma_start(out=out_rows[n * P : (n + 1) * P, :], in_=result[n][:])
@@ -191,10 +198,8 @@ def tile_gcn_pb_t_kernel(tc, x, ahat, gcn1_w, gcn1_b, out):
                     first_matmul(r, 2 * half + 1)
                 for n in banks[2 * half : 2 * half + 2]:
                     second_matmul(n)
-            vector_banks = [n for n in banks if first_active and n % 2 == 1]
             for n in banks:
-                if n not in vector_banks:
-                    relu_and_store(n, on_vector=False)
+                relu_and_store(n, on_gpsimd=(first_active and n % 2 == 1))
             if r + AHEAD < N_GROUPS:
                 transpose_x(r + AHEAD)
             if r < PASSES:
@@ -205,7 +210,5 @@ def tile_gcn_pb_t_kernel(tc, x, ahat, gcn1_w, gcn1_b, out):
                 a_codes[r] = quantise(a_grouped[:].rearrange("p j t -> p (j t)"), NODES, adjacency, "a")
             if first_active:
                 y_codes[r] = quantise(y_grouped[r][:].rearrange("p f t -> p (f t)"), D_HID, resident, "y")
-            for n in vector_banks:
-                relu_and_store(n, on_vector=True)
             if r + AHEAD < N_GROUPS:
                 x_codes[r + AHEAD] = quantise(x_grouped[r + AHEAD][:], GROUP, rotating, "x")

@@ -27,7 +27,7 @@ J_TILES = NODES // P
 N_BANKS = GRAPHS * J_TILES
 BANKS_PER_ROUND = N_BANKS // N_GROUPS
 AHEAD = 2
-LAG = 2
+LAG = 3
 
 FLOPS = 2 * GRAPHS * NODES * D_IN * D_HID + 2 * GRAPHS * NODES * NODES * D_HID
 
@@ -41,7 +41,7 @@ def tile_gcn_pb_t_kernel(tc, x, ahat, gcn1_w, gcn1_b, out):
         adjacency = stack.enter_context(tc.tile_pool(name="adjacency", bufs=PASSES))
         resident = stack.enter_context(tc.tile_pool(name="resident", bufs=N_GROUPS))
         rotating = stack.enter_context(tc.tile_pool(name="rotating", bufs=3))
-        results = stack.enter_context(tc.tile_pool(name="results", bufs=2 * BANKS_PER_ROUND))
+        results = stack.enter_context(tc.tile_pool(name="results", bufs=3 * BANKS_PER_ROUND))
         psum_xt = stack.enter_context(tc.psum_pool(name="psum_xt", bufs=2))
         psum_y = stack.enter_context(tc.psum_pool(name="psum_y", bufs=3))
         psum_out = stack.enter_context(tc.psum_pool(name="psum_out", bufs=3))
@@ -53,6 +53,7 @@ def tile_gcn_pb_t_kernel(tc, x, ahat, gcn1_w, gcn1_b, out):
         y_grouped = {}
         y_codes = {}
         a_raw = {}
+        a_grouped = {}
         a_codes = {}
         result = {}
 
@@ -163,16 +164,27 @@ def tile_gcn_pb_t_kernel(tc, x, ahat, gcn1_w, gcn1_b, out):
             nc.vector.tensor_tensor(out=biased[:], in0=out_bank[:], in1=bias_all[:], op=mybir.AluOpType.add)
             result[n] = biased
 
-        def relu_and_store(n, on_gpsimd):
-            if on_gpsimd:
-                nc.gpsimd.tensor_scalar(
-                    out=result[n][:],
-                    in0=result[n][:],
-                    scalar1=0.0,
-                    scalar2=0.0,
-                    op0=mybir.AluOpType.max,
-                    op1=mybir.AluOpType.add,
-                )
+        def regroup_adjacency(g, j_half):
+            if j_half == 0:
+                grouped = adjacency.tile([P, NODES, PACK], BF16, tag="a_grouped", align_bytes=64)
+                codes = adjacency.tile([P, NODES], U32, tag="a_codes", align_bytes=64)
+                scales = adjacency.tile([P, NODES], U8, tag="a_scales", align_bytes=64)
+                a_grouped[g] = grouped
+                a_codes[g] = (codes, scales)
+            j_cols = slice(j_half * (NODES // 2), (j_half + 1) * (NODES // 2))
+            regroup(a_grouped[g][:, j_cols, :], a_raw[g][:, :, j_cols])
+
+        def quantise_adjacency(g, j_half):
+            j_cols = slice(j_half * (NODES // 2), (j_half + 1) * (NODES // 2))
+            nc.vector.quantize_mx(
+                out=a_codes[g][0][:, j_cols].bitcast(FP8X4),
+                scales=a_codes[g][1][:, j_cols],
+                in_=a_grouped[g][:, j_cols, :].rearrange("p j t -> p (j t)"),
+            )
+
+        def relu_and_store(n, on_vector):
+            if on_vector:
+                nc.vector.tensor_scalar_max(out=result[n][:], in0=result[n][:], scalar1=0.0)
             else:
                 nc.scalar.activation(out=result[n][:], in_=result[n][:], func=mybir.ActivationFunctionType.Relu)
             nc.sync.dma_start(out=out_rows[n * P : (n + 1) * P, :], in_=result[n][:])
@@ -180,17 +192,23 @@ def tile_gcn_pb_t_kernel(tc, x, ahat, gcn1_w, gcn1_b, out):
         transpose_x(0)
         w_grouped = consts.tile([P, D_HID, PACK], BF16, tag="w_grouped", align_bytes=64)
         regroup(w_grouped[:], w_raw[:])
-        w_codes, w_scales = quantise(w_grouped[:].rearrange("p c t -> p (c t)"), D_HID, consts, "w")
         x_codes[0] = quantise(x_grouped[0][:], GROUP, rotating, "x")
+        w_codes, w_scales = quantise(w_grouped[:].rearrange("p c t -> p (c t)"), D_HID, consts, "w")
         transpose_x(1)
-        x_codes[1] = quantise(x_grouped[1][:], GROUP, rotating, "x")
         bias_bank = psum_out.tile([P, D_HID], F32, tag="out_bank")
         nc.tensor.matmul(out=bias_bank[:], lhsT=ones[:], rhs=bias_row[:], start=True, stop=True)
         bias_all = consts.tile([P, D_HID], F32, tag="bias_all")
         nc.scalar.copy(out=bias_all[:], in_=bias_bank[:])
 
+        fresh_pieces = []
         for r in range(N_GROUPS + LAG):
             first_active = r < N_GROUPS
+            if 1 <= r <= N_GROUPS:
+                y_codes[r - 1] = quantise(y_grouped[r - 1][:].rearrange("p f t -> p (f t)"), D_HID, resident, "y")
+            if r + 1 < N_GROUPS:
+                x_codes[r + 1] = quantise(x_grouped[r + 1][:], GROUP, rotating, "x")
+            for piece in fresh_pieces:
+                quantise_adjacency(*piece)
             banks = [BANKS_PER_ROUND * (r - LAG) + i for i in range(BANKS_PER_ROUND)] if r >= LAG else []
             for half in range(2):
                 if first_active:
@@ -199,16 +217,13 @@ def tile_gcn_pb_t_kernel(tc, x, ahat, gcn1_w, gcn1_b, out):
                 for n in banks[2 * half : 2 * half + 2]:
                     second_matmul(n)
             for n in banks:
-                relu_and_store(n, on_gpsimd=(first_active and n % 2 == 1))
+                relu_and_store(n, on_vector=(first_active and n % 2 == 1))
             if r + AHEAD < N_GROUPS:
                 transpose_x(r + AHEAD)
-            if r < PASSES:
-                a_grouped = adjacency.tile([P, NODES, PACK], BF16, tag="a_grouped", align_bytes=64)
-                for j_half in range(2):
-                    j_cols = slice(j_half * 512, (j_half + 1) * 512)
-                    regroup(a_grouped[:, j_cols, :], a_raw[r][:, :, j_cols])
-                a_codes[r] = quantise(a_grouped[:].rearrange("p j t -> p (j t)"), NODES, adjacency, "a")
-            if first_active:
-                y_codes[r] = quantise(y_grouped[r][:].rearrange("p f t -> p (f t)"), D_HID, resident, "y")
-            if r + AHEAD < N_GROUPS:
-                x_codes[r + AHEAD] = quantise(x_grouped[r + AHEAD][:], GROUP, rotating, "x")
+            fresh_pieces = []
+            if r == 0:
+                fresh_pieces = [(0, 0), (0, 1)]
+            if r == 1 or r == 2:
+                fresh_pieces = [(1, r - 1)]
+            for piece in fresh_pieces:
+                regroup_adjacency(*piece)

@@ -217,7 +217,7 @@ def tile_gcn_pb_t_kernel(tc, x, ahat, gcn1_w, gcn1_b, out):
                 for n in banks[2 * half : 2 * half + 2]:
                     second_matmul(n)
             for n in banks:
-                relu_and_store(n, on_vector=(first_active and n % 2 == 1))
+                relu_and_store(n, on_vector=(r + 1 < N_GROUPS and n % 2 == 1))
             if r + AHEAD < N_GROUPS:
                 transpose_x(r + AHEAD)
             fresh_pieces = []

@@ -12,6 +12,7 @@ FP8X4 = mybir.dt.float8_e4m3fn_x4
 P = 128
 PACK = 4
 K_PASS = P * PACK
+BANK_F32 = 512
 
 GRAPHS = 4
 NODES = 1024
@@ -21,11 +22,15 @@ D_HID = 512
 GROUP = K_PASS
 N_GROUPS = GRAPHS * NODES // GROUP
 PASSES = NODES // K_PASS
-F_CHUNK = 128
+WORDS = D_IN // 2
+WORD_HALVES = WORDS // P
+TILES_PER_BANK = BANK_F32 // WORDS
+F_CHUNK = BANK_F32 // PACK
 F_CHUNKS = D_HID // F_CHUNK
-J_TILES = NODES // P
-N_BANKS = GRAPHS * J_TILES
-BANKS_PER_ROUND = N_BANKS // N_GROUPS
+J_HALF = NODES // 2
+OUT_BANKS = GRAPHS * NODES // P
+BANKS_PER_GRAPH = NODES // P
+BANKS_PER_ROUND = OUT_BANKS // N_GROUPS
 AHEAD = 2
 LAG = 3
 
@@ -45,7 +50,6 @@ def tile_gcn_pb_t_kernel(tc, x, ahat, gcn1_w, gcn1_b, out):
         psum_xt = stack.enter_context(tc.psum_pool(name="psum_xt", bufs=2))
         psum_y = stack.enter_context(tc.psum_pool(name="psum_y", bufs=3))
         psum_out = stack.enter_context(tc.psum_pool(name="psum_out", bufs=3))
-        stack.enter_context(tc.manual_schedule())
 
         x_raw = {}
         x_grouped = {}
@@ -60,32 +64,33 @@ def tile_gcn_pb_t_kernel(tc, x, ahat, gcn1_w, gcn1_b, out):
         def load_x(g):
             raw = resident.tile([P, PACK * D_IN], BF16, tag="x_raw")
             nc.sync.dma_start(
-                out=raw[:], in_=x[g * GROUP : (g + 1) * GROUP, :].rearrange("(p t) k -> p (t k)", t=PACK)
+                out=raw[:], in_=x[g * GROUP : (g + 1) * GROUP, :].rearrange("(n t) k -> n (t k)", t=PACK)
             )
             x_raw[g] = raw
 
-        def load_adjacency(g):
+        def load_adjacency(i_pass):
             raw = adjacency.tile([P, PACK, NODES], BF16, tag="a_raw")
             nc.sync.dma_start(
-                out=raw[:], in_=ahat[g * K_PASS : (g + 1) * K_PASS, :].rearrange("(p t) j -> p t j", t=PACK)
+                out=raw[:],
+                in_=ahat[i_pass * K_PASS : (i_pass + 1) * K_PASS, :].rearrange("(p t) j -> p t j", t=PACK),
             )
-            a_raw[g] = raw
+            a_raw[i_pass] = raw
 
         bias_row = consts.tile([P, D_HID], BF16, tag="bias_row")
         nc.vector.memset(bias_row[:], 0.0)
 
         load_x(0)
         w_raw = consts.tile([P, PACK, D_HID], BF16, tag="w_raw")
-        for u in range(2):
+        for u in range(WORD_HALVES):
             nc.sync.dma_start(
                 out=w_raw[:, 2 * u : 2 * u + 2, :],
-                in_=gcn1_w[256 * u : 256 * (u + 1), :].rearrange("(q e) c -> q e c", e=2),
+                in_=gcn1_w[2 * P * u : 2 * P * (u + 1), :].rearrange("(q e) f -> q e f", e=2),
             )
         load_x(1)
         nc.sync.dma_start(out=bias_row[0:1, :], in_=gcn1_b.unsqueeze(0))
-        for g in range(PASSES):
-            load_adjacency(g)
-            load_x(AHEAD + g)
+        for i_pass in range(PASSES):
+            load_adjacency(i_pass)
+            load_x(AHEAD + i_pass)
         for g in range(AHEAD + PASSES, N_GROUPS):
             load_x(g)
 
@@ -112,26 +117,26 @@ def tile_gcn_pb_t_kernel(tc, x, ahat, gcn1_w, gcn1_b, out):
             words = x_raw[g][:].bitcast(F32)
             grouped = rotating.tile([P, PACK * GROUP], BF16, tag="x_grouped", align_bytes=64)
             grouped_words = grouped[:].bitcast(F32)
-            for pair in range(2):
-                xt = psum_xt.tile([P, 2, 2, P], F32, tag="xt")
-                for h in range(2):
-                    for u in range(2):
-                        first = (2 * pair + h) * 256 + u * P
+            for pair in range(PACK // TILES_PER_BANK):
+                xt = psum_xt.tile([P, TILES_PER_BANK, WORD_HALVES, P], F32, tag="xt")
+                for h in range(TILES_PER_BANK):
+                    for u in range(WORD_HALVES):
+                        first = (TILES_PER_BANK * pair + h) * WORDS + u * P
                         nc.tensor.transpose(xt[:, h, u, :], words[:, first : first + P], identity[:])
                 nc.scalar.copy(
-                    out=grouped_words[:, pair * 512 : (pair + 1) * 512].rearrange(
-                        "q (h n u) -> q h n u", h=2, n=P, u=2
+                    out=grouped_words[:, pair * BANK_F32 : (pair + 1) * BANK_F32].rearrange(
+                        "q (h n u) -> q h n u", h=TILES_PER_BANK, n=P, u=WORD_HALVES
                     ),
                     in_=xt[:].rearrange("q h u n -> q h n u"),
                 )
             x_grouped[g] = grouped
 
-        def first_matmul(g, c):
-            if c == 0:
+        def first_matmul(g, chunk):
+            if chunk == 0:
                 grouped = rotating.tile([P, D_HID, PACK], BF16, tag="y_grouped", align_bytes=64)
                 y_grouped[g] = grouped
             codes, scales = x_codes[g]
-            f_cols = slice(c * F_CHUNK, (c + 1) * F_CHUNK)
+            f_cols = slice(chunk * F_CHUNK, (chunk + 1) * F_CHUNK)
             y_bank = psum_y.tile([P, PACK, F_CHUNK], F32, tag="y_bank")
             for t in range(PACK):
                 n_cols = slice(t * P, (t + 1) * P)
@@ -146,54 +151,57 @@ def tile_gcn_pb_t_kernel(tc, x, ahat, gcn1_w, gcn1_b, out):
                 )
             nc.scalar.copy(out=y_grouped[g][:, f_cols, :], in_=y_bank[:].rearrange("n t f -> n f t"))
 
-        def second_matmul(n):
-            b = n // J_TILES
-            j_cols = slice((n % J_TILES) * P, (n % J_TILES + 1) * P)
+        def second_matmul(bank):
+            graph = bank // BANKS_PER_GRAPH
+            j_tile = bank % BANKS_PER_GRAPH
+            j_cols = slice(j_tile * P, (j_tile + 1) * P)
             out_bank = psum_out.tile([P, D_HID], F32, tag="out_bank")
-            for g in range(PASSES):
+            for i_pass in range(PASSES):
                 nc.tensor.matmul_mx(
                     out=out_bank[:],
-                    lhsT=a_codes[g][0][:, j_cols].bitcast(FP8X4),
-                    lhsT_scale=a_codes[g][1][:, j_cols],
-                    rhs=y_codes[PASSES * b + g][0][:].bitcast(FP8X4),
-                    rhs_scale=y_codes[PASSES * b + g][1][:],
-                    start=(g == 0),
-                    stop=(g == PASSES - 1),
+                    lhsT=a_codes[i_pass][0][:, j_cols].bitcast(FP8X4),
+                    lhsT_scale=a_codes[i_pass][1][:, j_cols],
+                    rhs=y_codes[PASSES * graph + i_pass][0][:].bitcast(FP8X4),
+                    rhs_scale=y_codes[PASSES * graph + i_pass][1][:],
+                    start=(i_pass == 0),
+                    stop=(i_pass == PASSES - 1),
                 )
             biased = results.tile([P, D_HID], F32, tag="result")
             nc.vector.tensor_tensor(out=biased[:], in0=out_bank[:], in1=bias_all[:], op=mybir.AluOpType.add)
-            result[n] = biased
+            result[bank] = biased
 
-        def regroup_adjacency(g, j_half):
+        def regroup_adjacency(i_pass, j_half):
             if j_half == 0:
                 grouped = adjacency.tile([P, NODES, PACK], BF16, tag="a_grouped", align_bytes=64)
                 codes = adjacency.tile([P, NODES], U32, tag="a_codes", align_bytes=64)
                 scales = adjacency.tile([P, NODES], U8, tag="a_scales", align_bytes=64)
-                a_grouped[g] = grouped
-                a_codes[g] = (codes, scales)
-            j_cols = slice(j_half * (NODES // 2), (j_half + 1) * (NODES // 2))
-            regroup(a_grouped[g][:, j_cols, :], a_raw[g][:, :, j_cols])
+                a_grouped[i_pass] = grouped
+                a_codes[i_pass] = (codes, scales)
+            j_cols = slice(j_half * J_HALF, (j_half + 1) * J_HALF)
+            regroup(a_grouped[i_pass][:, j_cols, :], a_raw[i_pass][:, :, j_cols])
 
-        def quantise_adjacency(g, j_half):
-            j_cols = slice(j_half * (NODES // 2), (j_half + 1) * (NODES // 2))
+        def quantise_adjacency(i_pass, j_half):
+            j_cols = slice(j_half * J_HALF, (j_half + 1) * J_HALF)
             nc.vector.quantize_mx(
-                out=a_codes[g][0][:, j_cols].bitcast(FP8X4),
-                scales=a_codes[g][1][:, j_cols],
-                in_=a_grouped[g][:, j_cols, :].rearrange("p j t -> p (j t)"),
+                out=a_codes[i_pass][0][:, j_cols].bitcast(FP8X4),
+                scales=a_codes[i_pass][1][:, j_cols],
+                in_=a_grouped[i_pass][:, j_cols, :].rearrange("p j t -> p (j t)"),
             )
 
-        def relu_and_store(n, on_vector):
+        def relu_and_store(bank, on_vector):
             if on_vector:
-                nc.vector.tensor_scalar_max(out=result[n][:], in0=result[n][:], scalar1=0.0)
+                nc.vector.tensor_scalar_max(out=result[bank][:], in0=result[bank][:], scalar1=0.0)
             else:
-                nc.scalar.activation(out=result[n][:], in_=result[n][:], func=mybir.ActivationFunctionType.Relu)
-            nc.sync.dma_start(out=out_rows[n * P : (n + 1) * P, :], in_=result[n][:])
+                nc.scalar.activation(
+                    out=result[bank][:], in_=result[bank][:], func=mybir.ActivationFunctionType.Relu
+                )
+            nc.sync.dma_start(out=out_rows[bank * P : (bank + 1) * P, :], in_=result[bank][:])
 
         transpose_x(0)
         w_grouped = consts.tile([P, D_HID, PACK], BF16, tag="w_grouped", align_bytes=64)
         regroup(w_grouped[:], w_raw[:])
         x_codes[0] = quantise(x_grouped[0][:], GROUP, rotating, "x")
-        w_codes, w_scales = quantise(w_grouped[:].rearrange("p c t -> p (c t)"), D_HID, consts, "w")
+        w_codes, w_scales = quantise(w_grouped[:].rearrange("p f t -> p (f t)"), D_HID, consts, "w")
         transpose_x(1)
         bias_bank = psum_out.tile([P, D_HID], F32, tag="out_bank")
         nc.tensor.matmul(out=bias_bank[:], lhsT=ones[:], rhs=bias_row[:], start=True, stop=True)
@@ -202,22 +210,21 @@ def tile_gcn_pb_t_kernel(tc, x, ahat, gcn1_w, gcn1_b, out):
 
         fresh_pieces = []
         for r in range(N_GROUPS + LAG):
-            first_active = r < N_GROUPS
             if 1 <= r <= N_GROUPS:
-                y_codes[r - 1] = quantise(y_grouped[r - 1][:].rearrange("p f t -> p (f t)"), D_HID, resident, "y")
+                y_codes[r - 1] = quantise(y_grouped[r - 1][:].rearrange("n f t -> n (f t)"), D_HID, resident, "y")
             if r + 1 < N_GROUPS:
                 x_codes[r + 1] = quantise(x_grouped[r + 1][:], GROUP, rotating, "x")
             for piece in fresh_pieces:
                 quantise_adjacency(*piece)
             banks = [BANKS_PER_ROUND * (r - LAG) + i for i in range(BANKS_PER_ROUND)] if r >= LAG else []
             for half in range(2):
-                if first_active:
+                if r < N_GROUPS:
                     first_matmul(r, 2 * half)
                     first_matmul(r, 2 * half + 1)
-                for n in banks[2 * half : 2 * half + 2]:
-                    second_matmul(n)
-            for n in banks:
-                relu_and_store(n, on_vector=(r + 1 < N_GROUPS and n % 2 == 1))
+                for bank in banks[2 * half : 2 * half + 2]:
+                    second_matmul(bank)
+            for bank in banks:
+                relu_and_store(bank, on_vector=(r + 1 < N_GROUPS and bank % 2 == 1))
             if r + AHEAD < N_GROUPS:
                 transpose_x(r + AHEAD)
             fresh_pieces = []

from contextlib import ExitStack

import concourse.mybir as mybir
from concourse.masks import make_identity

F32 = mybir.dt.float32
BF16 = mybir.dt.bfloat16
U32 = mybir.dt.uint32
U8 = mybir.dt.uint8
FP8X4 = mybir.dt.float8_e4m3fn_x4

P = 128
PACK = 4
K_PASS = P * PACK
BANK_F32 = 512

GRAPHS = 4
NODES = 1024
D_IN = 512
D_HID = 512

GROUP = K_PASS
N_GROUPS = GRAPHS * NODES // GROUP
PASSES = NODES // K_PASS
WORDS = D_IN // 2
WORD_HALVES = WORDS // P
TILES_PER_BANK = BANK_F32 // WORDS
F_CHUNK = BANK_F32 // PACK
F_CHUNKS = D_HID // F_CHUNK
J_HALF = NODES // 2
OUT_BANKS = GRAPHS * NODES // P
BANKS_PER_GRAPH = NODES // P
BANKS_PER_ROUND = OUT_BANKS // N_GROUPS
AHEAD = 2
LAG = 3

FLOPS = 2 * GRAPHS * NODES * D_IN * D_HID + 2 * GRAPHS * NODES * NODES * D_HID


def tile_gcn_pb_t_kernel(tc, x, ahat, gcn1_w, gcn1_b, out):
    nc = tc.nc
    out_rows = out.flatten_outer_dims()

    with ExitStack() as stack:
        consts = stack.enter_context(tc.tile_pool(name="consts", bufs=1))
        adjacency = stack.enter_context(tc.tile_pool(name="adjacency", bufs=PASSES))
        resident = stack.enter_context(tc.tile_pool(name="resident", bufs=N_GROUPS))
        rotating = stack.enter_context(tc.tile_pool(name="rotating", bufs=3))
        results = stack.enter_context(tc.tile_pool(name="results", bufs=3 * BANKS_PER_ROUND))
        psum_xt = stack.enter_context(tc.psum_pool(name="psum_xt", bufs=2))
        psum_y = stack.enter_context(tc.psum_pool(name="psum_y", bufs=3))
        psum_out = stack.enter_context(tc.psum_pool(name="psum_out", bufs=3))

        x_raw = {}
        x_grouped = {}
        x_codes = {}
        y_grouped = {}
        y_codes = {}
        a_raw = {}
        a_grouped = {}
        a_codes = {}
        result = {}

        def load_x(g):
            raw = resident.tile([P, PACK * D_IN], BF16, tag="x_raw")
            nc.sync.dma_start(
                out=raw[:], in_=x[g * GROUP : (g + 1) * GROUP, :].rearrange("(n t) k -> n (t k)", t=PACK)
            )
            x_raw[g] = raw

        def load_adjacency(i_pass):
            raw = adjacency.tile([P, PACK, NODES], BF16, tag="a_raw")
            nc.sync.dma_start(
                out=raw[:],
                in_=ahat[i_pass * K_PASS : (i_pass + 1) * K_PASS, :].rearrange("(p t) j -> p t j", t=PACK),
            )
            a_raw[i_pass] = raw

        bias_row = consts.tile([P, D_HID], BF16, tag="bias_row")
        nc.vector.memset(bias_row[:], 0.0)

        load_x(0)
        w_raw = consts.tile([P, PACK, D_HID], BF16, tag="w_raw")
        for u in range(WORD_HALVES):
            nc.sync.dma_start(
                out=w_raw[:, 2 * u : 2 * u + 2, :],
                in_=gcn1_w[2 * P * u : 2 * P * (u + 1), :].rearrange("(q e) f -> q e f", e=2),
            )
        load_x(1)
        nc.sync.dma_start(out=bias_row[0:1, :], in_=gcn1_b.unsqueeze(0))
        for i_pass in range(PASSES):
            load_adjacency(i_pass)
            load_x(AHEAD + i_pass)
        for g in range(AHEAD + PASSES, N_GROUPS):
            load_x(g)

        identity = consts.tile([P, P], F32, tag="identity")
        make_identity(nc, identity[:])
        ones = consts.tile([P, P], BF16, tag="ones")
        nc.vector.memset(ones[:], 1.0)
        warm = consts.tile([P, 1], F32, tag="warm")
        nc.vector.memset(warm[:], 0.0)
        nc.scalar.activation(out=warm[:], in_=warm[:], func=mybir.ActivationFunctionType.Relu)

        def regroup(dst, src):
            nc.vector.tensor_copy(
                out=dst.rearrange("p (c i) t -> p c t i", i=4), in_=src.rearrange("p t (c i) -> p c t i", i=4)
            )

        def quantise(grouped, width, pool, tag):
            codes = pool.tile([P, width], U32, tag=tag + "_codes", align_bytes=64)
            scales = pool.tile([P, width], U8, tag=tag + "_scales", align_bytes=64)
            nc.vector.quantize_mx(out=codes[:].bitcast(FP8X4), scales=scales[:], in_=grouped)
            return codes, scales

        def transpose_x(g):
            words = x_raw[g][:].bitcast(F32)
            grouped = rotating.tile([P, PACK * GROUP], BF16, tag="x_grouped", align_bytes=64)
            grouped_words = grouped[:].bitcast(F32)
            for pair in range(PACK // TILES_PER_BANK):
                xt = psum_xt.tile([P, TILES_PER_BANK, WORD_HALVES, P], F32, tag="xt")
                for h in range(TILES_PER_BANK):
                    for u in range(WORD_HALVES):
                        first = (TILES_PER_BANK * pair + h) * WORDS + u * P
                        nc.tensor.transpose(xt[:, h, u, :], words[:, first : first + P], identity[:])
                nc.scalar.copy(
                    out=grouped_words[:, pair * BANK_F32 : (pair + 1) * BANK_F32].rearrange(
                        "q (h n u) -> q h n u", h=TILES_PER_BANK, n=P, u=WORD_HALVES
                    ),
                    in_=xt[:].rearrange("q h u n -> q h n u"),
                )
            x_grouped[g] = grouped

        def first_matmul(g, chunk):
            if chunk == 0:
                grouped = rotating.tile([P, D_HID, PACK], BF16, tag="y_grouped", align_bytes=64)
                y_grouped[g] = grouped
            codes, scales = x_codes[g]
            f_cols = slice(chunk * F_CHUNK, (chunk + 1) * F_CHUNK)
            y_bank = psum_y.tile([P, PACK, F_CHUNK], F32, tag="y_bank")
            for t in range(PACK):
                n_cols = slice(t * P, (t + 1) * P)
                nc.tensor.matmul_mx(
                    out=y_bank[:, t, :],
                    lhsT=codes[:, n_cols].bitcast(FP8X4),
                    lhsT_scale=scales[:, n_cols],
                    rhs=w_codes[:, f_cols].bitcast(FP8X4),
                    rhs_scale=w_scales[:, f_cols],
                    start=True,
                    stop=True,
                )
            nc.scalar.copy(out=y_grouped[g][:, f_cols, :], in_=y_bank[:].rearrange("n t f -> n f t"))

        def second_matmul(bank):
            graph = bank // BANKS_PER_GRAPH
            j_tile = bank % BANKS_PER_GRAPH
            j_cols = slice(j_tile * P, (j_tile + 1) * P)
            out_bank = psum_out.tile([P, D_HID], F32, tag="out_bank")
            for i_pass in range(PASSES):
                nc.tensor.matmul_mx(
                    out=out_bank[:],
                    lhsT=a_codes[i_pass][0][:, j_cols].bitcast(FP8X4),
                    lhsT_scale=a_codes[i_pass][1][:, j_cols],
                    rhs=y_codes[PASSES * graph + i_pass][0][:].bitcast(FP8X4),
                    rhs_scale=y_codes[PASSES * graph + i_pass][1][:],
                    start=(i_pass == 0),
                    stop=(i_pass == PASSES - 1),
                )
            biased = results.tile([P, D_HID], F32, tag="result")
            nc.vector.tensor_tensor(out=biased[:], in0=out_bank[:], in1=bias_all[:], op=mybir.AluOpType.add)
            result[bank] = biased

        def regroup_adjacency(i_pass, j_half):
            if j_half == 0:
                grouped = adjacency.tile([P, NODES, PACK], BF16, tag="a_grouped", align_bytes=64)
                codes = adjacency.tile([P, NODES], U32, tag="a_codes", align_bytes=64)
                scales = adjacency.tile([P, NODES], U8, tag="a_scales", align_bytes=64)
                a_grouped[i_pass] = grouped
                a_codes[i_pass] = (codes, scales)
            j_cols = slice(j_half * J_HALF, (j_half + 1) * J_HALF)
            regroup(a_grouped[i_pass][:, j_cols, :], a_raw[i_pass][:, :, j_cols])

        def quantise_adjacency(i_pass, j_half):
            j_cols = slice(j_half * J_HALF, (j_half + 1) * J_HALF)
            nc.vector.quantize_mx(
                out=a_codes[i_pass][0][:, j_cols].bitcast(FP8X4),
                scales=a_codes[i_pass][1][:, j_cols],
                in_=a_grouped[i_pass][:, j_cols, :].rearrange("p j t -> p (j t)"),
            )

        def relu_and_store(bank, on_vector):
            if on_vector:
                nc.vector.tensor_scalar_max(out=result[bank][:], in0=result[bank][:], scalar1=0.0)
            else:
                nc.scalar.activation(
                    out=result[bank][:], in_=result[bank][:], func=mybir.ActivationFunctionType.Relu
                )
            nc.sync.dma_start(out=out_rows[bank * P : (bank + 1) * P, :], in_=result[bank][:])

        transpose_x(0)
        w_grouped = consts.tile([P, D_HID, PACK], BF16, tag="w_grouped", align_bytes=64)
        regroup(w_grouped[:], w_raw[:])
        x_codes[0] = quantise(x_grouped[0][:], GROUP, rotating, "x")
        w_codes, w_scales = quantise(w_grouped[:].rearrange("p f t -> p (f t)"), D_HID, consts, "w")
        transpose_x(1)
        bias_bank = psum_out.tile([P, D_HID], F32, tag="out_bank")
        nc.tensor.matmul(out=bias_bank[:], lhsT=ones[:], rhs=bias_row[:], start=True, stop=True)
        bias_all = consts.tile([P, D_HID], F32, tag="bias_all")
        nc.scalar.copy(out=bias_all[:], in_=bias_bank[:])

        fresh_pieces = []
        for r in range(N_GROUPS + LAG):
            if 1 <= r <= N_GROUPS:
                y_codes[r - 1] = quantise(y_grouped[r - 1][:].rearrange("n f t -> n (f t)"), D_HID, resident, "y")
            if r + 1 < N_GROUPS:
                x_codes[r + 1] = quantise(x_grouped[r + 1][:], GROUP, rotating, "x")
            for piece in fresh_pieces:
                quantise_adjacency(*piece)
            banks = [BANKS_PER_ROUND * (r - LAG) + i for i in range(BANKS_PER_ROUND)] if r >= LAG else []
            for half in range(2):
                if r < N_GROUPS:
                    first_matmul(r, 2 * half)
                    first_matmul(r, 2 * half + 1)
                for bank in banks[2 * half : 2 * half + 2]:
                    second_matmul(bank)
            for bank in banks:
                relu_and_store(bank, on_vector=(r + 1 < N_GROUPS and bank % 2 == 1))
            if r + AHEAD < N_GROUPS:
                transpose_x(r + AHEAD)
            fresh_pieces = []
            if r == 0:
                fresh_pieces = [(0, 0), (0, 1)]
            if r == 1 or r == 2:
                fresh_pieces = [(1, r - 1)]
            for piece in fresh_pieces:
                regroup_adjacency(*piece)
